import numpy as np
import ml_dtypes

BF16 = ml_dtypes.bfloat16


def bf(x):
    return np.asarray(x, np.float32).astype(BF16)


def f32(x):
    return np.asarray(x, np.float32)


def f64(x):
    return np.asarray(x).astype(np.float64)


def striped(idx):
    return np.tile(idx.reshape(-1, 16).T, (8, 1))


KC, DD, C, S, H, MN, N = 8, 32, 256, 1024, 512, 4, 2048


def setup_inputs():
    v = np.abs(np.random.standard_normal((KC, DD, S)))
    t = (v / np.sqrt((v ** 2).sum(axis=1, keepdims=True))).reshape(C, S)
    raw = 1.0 + 0.1 * np.random.standard_normal((1,))
    idx = np.concatenate([np.random.permutation(S)[:H] for _ in range(MN)])
    return {"t": f32(t), "raw_param": f32(raw), "offs": striped(idx)}


def reference(t, raw_param, offs):
    idx = offs[:16].T.reshape(-1)
    t = f64(t)
    p = 1.0 / (1.0 + np.exp(-f64(raw_param)[0]))
    z = t[:, idx].reshape(C, MN, H)
    u1 = z.sum(axis=1) / MN
    u2 = z.sum(axis=1) / KC
    return p * u1 + (1.0 - p) * u2 + t[:, :H]

@@ -1,0 +1,50 @@
+import concourse.mybir as mybir
+
+F32 = mybir.dt.float32
+U16 = mybir.dt.uint16
+ADD = mybir.AluOpType.add
+MULT = mybir.AluOpType.mult
+ACT = mybir.ActivationFunctionType
+
+P = 128
+C = 256
+S = 1024
+H = 512
+MN = 4
+KC = 8
+N = MN * H
+PIECE = H // 16
+
+
+def tile_capsulenet_kernel(tc, t, raw_param, offs, out):
+    nc = tc.nc
+    with (
+        tc.tile_pool(name="held", bufs=1) as held,
+        tc.tile_pool(name="blocks", bufs=2) as blocks,
+        tc.tile_pool(name="sums", bufs=4) as sums,
+    ):
+        offsets = held.tile([P, N // 16], U16, name="offsets")
+        nc.sync.dma_start(offsets[:], offs)
+
+        raw = held.tile([P, 1], F32, name="raw")
+        nc.scalar.dma_start(raw[:], raw_param.partition_broadcast(P))
+        p = held.tile([P, 1], F32, name="p")
+        nc.scalar.activation(p[:], raw[:], ACT.Sigmoid)
+        w = held.tile([P, 1], F32, name="w")
+        nc.vector.tensor_scalar(w[:], p[:], 1.0 / MN - 1.0 / KC, 1.0 / KC, MULT, ADD)
+
+        for b in range(C // P):
+            rows = slice(b * P, (b + 1) * P)
+            plain = blocks.tile([P, S], F32, name="plain")
+            nc.sync.dma_start(plain[:], t[rows, :])
+
+            weighted = blocks.tile([P, S], F32, name="weighted")
+            nc.scalar.activation(weighted[:], plain[:], ACT.Copy, scale=w[:])
+
+            so_far = plain[:, 0:H]
+            for m in range(MN):
+                picked = weighted[:].indirect(offsets[:, m * PIECE : (m + 1) * PIECE])
+                total = sums.tile([P, H], F32, name="total")
+                nc.vector.tensor_tensor(total[:], picked, so_far, ADD)
+                so_far = total[:]
+            nc.sync.dma_start(out[rows, :], so_far)

@@ -13,7 +13,8 @@ H = 512
 MN = 4
 KC = 8
 N = MN * H
-PIECE = H // 16
+HALVES = 2
+Q = H // HALVES
 
 
 def tile_capsulenet_kernel(tc, t, raw_param, offs, out):
@@ -41,10 +42,15 @@ def tile_capsulenet_kernel(tc, t, raw_param, offs, out):
             weighted = blocks.tile([P, S], F32, name="weighted")
             nc.scalar.activation(weighted[:], plain[:], ACT.Copy, scale=w[:])
 
-            so_far = plain[:, 0:H]
+            so_far = plain
             for m in range(MN):
-                picked = weighted[:].indirect(offsets[:, m * PIECE : (m + 1) * PIECE])
                 total = sums.tile([P, H], F32, name="total")
-                nc.vector.tensor_tensor(total[:], picked, so_far, ADD)
-                so_far = total[:]
-            nc.sync.dma_start(out[rows, :], so_far)
+                for h in range(HALVES):
+                    first = (m * H + h * Q) // 16
+                    picked = weighted[:].indirect(offsets[:, first : first + Q // 16])
+                    nodes = slice(h * Q, (h + 1) * Q)
+                    nc.vector.tensor_tensor(total[:, nodes], picked, so_far[:, nodes], ADD)
+                so_far = total
+            for h in range(HALVES):
+                nodes = slice(h * Q, (h + 1) * Q)
+                nc.sync.dma_start(out[rows, nodes], so_far[:, nodes])

@@ -36,11 +36,17 @@ def tile_capsulenet_kernel(tc, t, raw_param, offs, out):
 
         for b in range(C // P):
             rows = slice(b * P, (b + 1) * P)
+            left, right = slice(0, S // 2), slice(S // 2, S)
             plain = blocks.tile([P, S], F32, name="plain")
-            nc.sync.dma_start(plain[:], t[rows, :])
+            nc.scalar.dma_start(plain[:, left], t[rows, left])
+            nc.sync.dma_start(plain[:, right], t[rows, right])
 
             weighted = blocks.tile([P, S], F32, name="weighted")
-            nc.scalar.activation(weighted[:], plain[:], ACT.Copy, scale=w[:])
+            if b == 0:
+                nc.vector.tensor_scalar(weighted[:, left], plain[:, left], w[:], None, MULT)
+                nc.vector.tensor_scalar(weighted[:, right], plain[:, right], w[:], None, MULT)
+            else:
+                nc.scalar.activation(weighted[:], plain[:], ACT.Copy, scale=w[:])
 
             so_far = plain
             for m in range(MN):

@@ -25,7 +25,6 @@ def tile_capsulenet_kernel(tc, t, raw_param, offs, out):
         tc.tile_pool(name="sums", bufs=4) as sums,
     ):
         offsets = held.tile([P, N // 16], U16, name="offsets")
-        nc.sync.dma_start(offsets[:], offs)
 
         raw = held.tile([P, 1], F32, name="raw")
         nc.scalar.dma_start(raw[:], raw_param.partition_broadcast(P))
@@ -36,15 +35,14 @@ def tile_capsulenet_kernel(tc, t, raw_param, offs, out):
 
         for b in range(C // P):
             rows = slice(b * P, (b + 1) * P)
-            left, right = slice(0, S // 2), slice(S // 2, S)
             plain = blocks.tile([P, S], F32, name="plain")
-            nc.scalar.dma_start(plain[:, left], t[rows, left])
-            nc.sync.dma_start(plain[:, right], t[rows, right])
+            nc.sync.dma_start(plain[:], t[rows, :])
+            if b == 0:
+                nc.sync.dma_start(offsets[:], offs)
 
             weighted = blocks.tile([P, S], F32, name="weighted")
             if b == 0:
-                nc.vector.tensor_scalar(weighted[:, left], plain[:, left], w[:], None, MULT)
-                nc.vector.tensor_scalar(weighted[:, right], plain[:, right], w[:], None, MULT)
+                nc.vector.tensor_scalar(weighted[:], plain[:], w[:], None, MULT)
             else:
                 nc.scalar.activation(weighted[:], plain[:], ACT.Copy, scale=w[:])
 

@@ -35,14 +35,17 @@ def tile_capsulenet_kernel(tc, t, raw_param, offs, out):
 
         for b in range(C // P):
             rows = slice(b * P, (b + 1) * P)
+            left, right = slice(0, S // 2), slice(S // 2, S)
             plain = blocks.tile([P, S], F32, name="plain")
-            nc.sync.dma_start(plain[:], t[rows, :])
+            nc.sync.dma_start(plain[:, left], t[rows, left])
+            nc.sync.dma_start(plain[:, right], t[rows, right])
             if b == 0:
                 nc.sync.dma_start(offsets[:], offs)
 
             weighted = blocks.tile([P, S], F32, name="weighted")
             if b == 0:
-                nc.vector.tensor_scalar(weighted[:], plain[:], w[:], None, MULT)
+                nc.vector.tensor_scalar(weighted[:, left], plain[:, left], w[:], None, MULT)
+                nc.vector.tensor_scalar(weighted[:, right], plain[:, right], w[:], None, MULT)
             else:
                 nc.scalar.activation(weighted[:], plain[:], ACT.Copy, scale=w[:])
 

@@ -19,10 +19,12 @@ Q = H // HALVES
 
 def tile_capsulenet_kernel(tc, t, raw_param, offs, out):
     nc = tc.nc
+    halves = [slice(h * Q, (h + 1) * Q) for h in range(HALVES)]
+    left, right = slice(0, S // 2), slice(S // 2, S)
     with (
         tc.tile_pool(name="held", bufs=1) as held,
         tc.tile_pool(name="blocks", bufs=2) as blocks,
-        tc.tile_pool(name="sums", bufs=4) as sums,
+        tc.tile_pool(name="sums", bufs=MN + 1) as sums,
     ):
         offsets = held.tile([P, N // 16], U16, name="offsets")
 
@@ -32,32 +34,40 @@ def tile_capsulenet_kernel(tc, t, raw_param, offs, out):
         nc.scalar.activation(p[:], raw[:], ACT.Sigmoid)
         w = held.tile([P, 1], F32, name="w")
         nc.vector.tensor_scalar(w[:], p[:], 1.0 / MN - 1.0 / KC, 1.0 / KC, MULT, ADD)
+        one_over_w = held.tile([P, 1], F32, name="one_over_w")
+        nc.vector.reciprocal(one_over_w[:], w[:])
 
         for b in range(C // P):
             rows = slice(b * P, (b + 1) * P)
-            left, right = slice(0, S // 2), slice(S // 2, S)
             plain = blocks.tile([P, S], F32, name="plain")
             nc.sync.dma_start(plain[:, left], t[rows, left])
-            nc.sync.dma_start(plain[:, right], t[rows, right])
             if b == 0:
                 nc.sync.dma_start(offsets[:], offs)
+            nc.sync.dma_start(plain[:, right], t[rows, right])
 
-            weighted = blocks.tile([P, S], F32, name="weighted")
             if b == 0:
-                nc.vector.tensor_scalar(weighted[:, left], plain[:, left], w[:], None, MULT)
-                nc.vector.tensor_scalar(weighted[:, right], plain[:, right], w[:], None, MULT)
+                window = plain
+                so_far = sums.tile([P, H], F32, name="total")
+                for nodes in halves:
+                    nc.vector.tensor_scalar(so_far[:, nodes], plain[:, nodes], one_over_w[:], None, MULT)
             else:
-                nc.scalar.activation(weighted[:], plain[:], ACT.Copy, scale=w[:])
+                window = blocks.tile([P, S], F32, name="weighted")
+                nc.scalar.activation(window[:], plain[:], ACT.Copy, scale=w[:])
+                so_far = plain
 
-            so_far = plain
             for m in range(MN):
                 total = sums.tile([P, H], F32, name="total")
-                for h in range(HALVES):
+                for h, nodes in enumerate(halves):
                     first = (m * H + h * Q) // 16
-                    picked = weighted[:].indirect(offsets[:, first : first + Q // 16])
-                    nodes = slice(h * Q, (h + 1) * Q)
+                    picked = window[:].indirect(offsets[:, first : first + Q // 16])
                     nc.vector.tensor_tensor(total[:, nodes], picked, so_far[:, nodes], ADD)
                 so_far = total
-            for h in range(HALVES):
-                nodes = slice(h * Q, (h + 1) * Q)
-                nc.sync.dma_start(out[rows, nodes], so_far[:, nodes])
+
+            if b == 0:
+                result = blocks.tile([P, H], F32, name="result")
+                for nodes in halves:
+                    nc.scalar.activation(result[:, nodes], so_far[:, nodes], ACT.Copy, scale=w[:])
+            else:
+                result = so_far
+            for nodes in halves:
+                nc.sync.dma_start(out[rows, nodes], result[:, nodes])

@@ -13,21 +13,15 @@ H = 512
 MN = 4
 KC = 8
 N = MN * H
-HALVES = 2
-Q = H // HALVES
 
 
 def tile_capsulenet_kernel(tc, t, raw_param, offs, out):
     nc = tc.nc
-    halves = [slice(h * Q, (h + 1) * Q) for h in range(HALVES)]
     left, right = slice(0, S // 2), slice(S // 2, S)
     with (
         tc.tile_pool(name="held", bufs=1) as held,
-        tc.tile_pool(name="blocks", bufs=2) as blocks,
-        tc.tile_pool(name="sums", bufs=MN + 1) as sums,
+        tc.tile_pool(name="sums", bufs=6) as sums,
     ):
-        offsets = held.tile([P, N // 16], U16, name="offsets")
-
         raw = held.tile([P, 1], F32, name="raw")
         nc.scalar.dma_start(raw[:], raw_param.partition_broadcast(P))
         p = held.tile([P, 1], F32, name="p")
@@ -37,37 +31,42 @@ def tile_capsulenet_kernel(tc, t, raw_param, offs, out):
         one_over_w = held.tile([P, 1], F32, name="one_over_w")
         nc.vector.reciprocal(one_over_w[:], w[:])
 
-        for b in range(C // P):
-            rows = slice(b * P, (b + 1) * P)
-            plain = blocks.tile([P, S], F32, name="plain")
-            nc.sync.dma_start(plain[:, left], t[rows, left])
-            if b == 0:
-                nc.sync.dma_start(offsets[:], offs)
-            nc.sync.dma_start(plain[:, right], t[rows, right])
+        offsets = held.tile([P, N // 16], U16, name="offsets")
+        plain_a = held.tile([P, S], F32, name="plain_a")
+        plain_b = held.tile([P, S], F32, name="plain_b")
+        nc.sync.dma_start(offsets[:], offs)
+        nc.sync.dma_start(plain_a[:, left], t[0:P, left])
+        nc.sync.dma_start(plain_a[:, right], t[0:P, right])
+        nc.sync.dma_start(plain_b[:, left], t[P:C, left])
+        nc.sync.dma_start(plain_b[:, right], t[P:C, right])
 
-            if b == 0:
-                window = plain
-                so_far = sums.tile([P, H], F32, name="total")
-                for nodes in halves:
-                    nc.vector.tensor_scalar(so_far[:, nodes], plain[:, nodes], one_over_w[:], None, MULT)
-            else:
-                window = blocks.tile([P, S], F32, name="weighted")
-                nc.scalar.activation(window[:], plain[:], ACT.Copy, scale=w[:])
-                so_far = plain
+        def add_neighbour(window, so_far, m, pieces):
+            total = sums.tile([P, H], F32, name="total")
+            width = H // pieces
+            for i in range(pieces):
+                nodes = slice(i * width, (i + 1) * width)
+                first = (m * H + i * width) // 16
+                picked = window[:].indirect(offsets[:, first : first + width // 16])
+                nc.vector.tensor_tensor(total[:, nodes], picked, so_far[:, nodes], ADD)
+            return total
 
-            for m in range(MN):
-                total = sums.tile([P, H], F32, name="total")
-                for h, nodes in enumerate(halves):
-                    first = (m * H + h * Q) // 16
-                    picked = window[:].indirect(offsets[:, first : first + Q // 16])
-                    nc.vector.tensor_tensor(total[:, nodes], picked, so_far[:, nodes], ADD)
-                so_far = total
+        sum_a = sums.tile([P, H], F32, name="total")
+        nc.vector.tensor_scalar(sum_a[:], plain_a[:, 0:H], one_over_w[:], None, MULT)
+        weighted_b = held.tile([P, S], F32, name="weighted_b")
+        nc.scalar.activation(weighted_b[:], plain_b[:], ACT.Copy, scale=w[:])
+        sum_b = plain_b
 
-            if b == 0:
-                result = blocks.tile([P, H], F32, name="result")
-                for nodes in halves:
-                    nc.scalar.activation(result[:, nodes], so_far[:, nodes], ACT.Copy, scale=w[:])
-            else:
-                result = so_far
-            for nodes in halves:
-                nc.sync.dma_start(out[rows, nodes], result[:, nodes])
+        for m in range(MN // 2):
+            sum_a = add_neighbour(plain_a, sum_a, m, pieces=2)
+        for m in range(MN // 2):
+            sum_b = add_neighbour(weighted_b, sum_b, m, pieces=1)
+            sum_a = add_neighbour(plain_a, sum_a, MN // 2 + m, pieces=1)
+        result_a = held.tile([P, H], F32, name="result_a")
+        halves = (slice(0, H // 2), slice(H // 2, H))
+        for nodes in halves:
+            nc.scalar.activation(result_a[:, nodes], sum_a[:, nodes], ACT.Copy, scale=w[:])
+            nc.scalar.dma_start(out[0:P, nodes], result_a[:, nodes])
+        for m in range(MN // 2, MN):
+            sum_b = add_neighbour(weighted_b, sum_b, m, pieces=2)
+        for nodes in halves:
+            nc.sync.dma_start(out[P:C, nodes], sum_b[:, nodes])

@@ -35,8 +35,9 @@ def tile_capsulenet_kernel(tc, t, raw_param, offs, out):
         plain_a = held.tile([P, S], F32, name="plain_a")
         plain_b = held.tile([P, S], F32, name="plain_b")
         nc.sync.dma_start(offsets[:], offs)
-        nc.sync.dma_start(plain_a[:, left], t[0:P, left])
-        nc.sync.dma_start(plain_a[:, right], t[0:P, right])
+        for k in range(4):
+            columns = slice(k * S // 4, (k + 1) * S // 4)
+            nc.sync.dma_start(plain_a[:, columns], t[0:P, columns])
         nc.sync.dma_start(plain_b[:, left], t[P:C, left])
         nc.sync.dma_start(plain_b[:, right], t[P:C, right])
 

@@ -54,7 +54,8 @@ def tile_capsulenet_kernel(tc, t, raw_param, offs, out):
         sum_a = sums.tile([P, H], F32, name="total")
         nc.vector.tensor_scalar(sum_a[:], plain_a[:, 0:H], one_over_w[:], None, MULT)
         weighted_b = held.tile([P, S], F32, name="weighted_b")
-        nc.scalar.activation(weighted_b[:], plain_b[:], ACT.Copy, scale=w[:])
+        for columns in (left, right):
+            nc.scalar.activation(weighted_b[:, columns], plain_b[:, columns], ACT.Copy, scale=w[:])
         sum_b = plain_b
 
         for m in range(MN // 2):

@@ -41,15 +41,20 @@ def tile_capsulenet_kernel(tc, t, raw_param, offs, out):
         nc.sync.dma_start(plain_b[:, left], t[P:C, left])
         nc.sync.dma_start(plain_b[:, right], t[P:C, right])
 
-        def add_neighbour(window, so_far, m, pieces):
+        def add_neighbour(window, so_far, m, widths):
             total = sums.tile([P, H], F32, name="total")
-            width = H // pieces
-            for i in range(pieces):
-                nodes = slice(i * width, (i + 1) * width)
-                first = (m * H + i * width) // 16
+            start = 0
+            for width in widths:
+                nodes = slice(start, start + width)
+                first = (m * H + start) // 16
                 picked = window[:].indirect(offsets[:, first : first + width // 16])
                 nc.vector.tensor_tensor(total[:, nodes], picked, so_far[:, nodes], ADD)
+                start += width
             return total
+
+        whole = (H,)
+        two = (H // 2, H // 2)
+        tapered = (H // 2, 3 * H // 8, H // 8)
 
         sum_a = sums.tile([P, H], F32, name="total")
         nc.vector.tensor_scalar(sum_a[:], plain_a[:, 0:H], one_over_w[:], None, MULT)
@@ -59,16 +64,19 @@ def tile_capsulenet_kernel(tc, t, raw_param, offs, out):
         sum_b = plain_b
 
         for m in range(MN // 2):
-            sum_a = add_neighbour(plain_a, sum_a, m, pieces=2)
+            sum_a = add_neighbour(plain_a, sum_a, m, two)
         for m in range(MN // 2):
-            sum_b = add_neighbour(weighted_b, sum_b, m, pieces=1)
-            sum_a = add_neighbour(plain_a, sum_a, MN // 2 + m, pieces=1)
+            sum_b = add_neighbour(weighted_b, sum_b, m, whole)
+            sum_a = add_neighbour(plain_a, sum_a, MN // 2 + m, whole)
         result_a = held.tile([P, H], F32, name="result_a")
         halves = (slice(0, H // 2), slice(H // 2, H))
         for nodes in halves:
             nc.scalar.activation(result_a[:, nodes], sum_a[:, nodes], ACT.Copy, scale=w[:])
             nc.scalar.dma_start(out[0:P, nodes], result_a[:, nodes])
-        for m in range(MN // 2, MN):
-            sum_b = add_neighbour(weighted_b, sum_b, m, pieces=2)
-        for nodes in halves:
+        sum_b = add_neighbour(weighted_b, sum_b, MN - 2, two)
+        sum_b = add_neighbour(weighted_b, sum_b, MN - 1, tapered)
+        start = 0
+        for width in tapered:
+            nodes = slice(start, start + width)
             nc.sync.dma_start(out[P:C, nodes], sum_b[:, nodes])
+            start += width

@@ -54,7 +54,7 @@ def tile_capsulenet_kernel(tc, t, raw_param, offs, out):
 
         whole = (H,)
         two = (H // 2, H // 2)
-        tapered = (H // 2, 3 * H // 8, H // 8)
+        tapered = (H // 2, H // 4, H // 4)
 
         sum_a = sums.tile([P, H], F32, name="total")
         nc.vector.tensor_scalar(sum_a[:], plain_a[:, 0:H], one_over_w[:], None, MULT)

@@ -1,9 +1,9 @@
 import concourse.mybir as mybir
+from concourse.masks import make_identity
 
 F32 = mybir.dt.float32
 U16 = mybir.dt.uint16
 ADD = mybir.AluOpType.add
-MULT = mybir.AluOpType.mult
 ACT = mybir.ActivationFunctionType
 
 P = 128
@@ -13,6 +13,7 @@ H = 512
 MN = 4
 KC = 8
 N = MN * H
+FLOPS = C * H * (MN + 2)
 
 
 def tile_capsulenet_kernel(tc, t, raw_param, offs, out):
@@ -21,16 +22,10 @@ def tile_capsulenet_kernel(tc, t, raw_param, offs, out):
     with (
         tc.tile_pool(name="held", bufs=1) as held,
         tc.tile_pool(name="sums", bufs=6) as sums,
+        tc.psum_pool(name="psum", bufs=1) as psum,
     ):
         raw = held.tile([P, 1], F32, name="raw")
         nc.scalar.dma_start(raw[:], raw_param.partition_broadcast(P))
-        p = held.tile([P, 1], F32, name="p")
-        nc.scalar.activation(p[:], raw[:], ACT.Sigmoid)
-        w = held.tile([P, 1], F32, name="w")
-        nc.vector.tensor_scalar(w[:], p[:], 1.0 / MN - 1.0 / KC, 1.0 / KC, MULT, ADD)
-        one_over_w = held.tile([P, 1], F32, name="one_over_w")
-        nc.vector.reciprocal(one_over_w[:], w[:])
-
         offsets = held.tile([P, N // 16], U16, name="offsets")
         plain_a = held.tile([P, S], F32, name="plain_a")
         plain_b = held.tile([P, S], F32, name="plain_b")
@@ -40,6 +35,24 @@ def tile_capsulenet_kernel(tc, t, raw_param, offs, out):
             nc.sync.dma_start(plain_a[:, columns], t[0:P, columns])
         nc.sync.dma_start(plain_b[:, left], t[P:C, left])
         nc.sync.dma_start(plain_b[:, right], t[P:C, right])
+
+        identity = held.tile([P, P], F32, name="identity")
+        make_identity(nc, identity[:])
+
+        slope = 1.0 / MN - 1.0 / KC
+        p = held.tile([P, 1], F32, name="p")
+        nc.scalar.activation(p[:], raw[:], ACT.Sigmoid)
+        w = held.tile([P, 1], F32, name="w")
+        nc.scalar.activation(w[:], p[:], ACT.Copy, scale=slope, bias=1.0 / KC)
+        weighted_b = held.tile([P, S], F32, name="weighted_b")
+        for columns in (left, right):
+            nc.scalar.activation(weighted_b[:, columns], plain_b[:, columns], ACT.Copy, scale=w[:])
+        rest = held.tile([P, 1], F32, name="rest")
+        nc.scalar.activation(rest[:], p[:], ACT.Copy, scale=-2.0 * slope, bias=1.0 - 2.0 / KC)
+        diagonal_w = held.tile([P, P], F32, name="diagonal_w")
+        nc.scalar.activation(diagonal_w[:], identity[:], ACT.Copy, scale=w[:])
+        diagonal_rest = held.tile([P, P], F32, name="diagonal_rest")
+        nc.scalar.activation(diagonal_rest[:], identity[:], ACT.Copy, scale=rest[:])
 
         def add_neighbour(window, so_far, m, widths):
             total = sums.tile([P, H], F32, name="total")
@@ -56,22 +69,25 @@ def tile_capsulenet_kernel(tc, t, raw_param, offs, out):
         two = (H // 2, H // 2)
         tapered = (H // 2, H // 4, H // 4)
 
-        sum_a = sums.tile([P, H], F32, name="total")
-        nc.vector.tensor_scalar(sum_a[:], plain_a[:, 0:H], one_over_w[:], None, MULT)
-        weighted_b = held.tile([P, S], F32, name="weighted_b")
-        for columns in (left, right):
-            nc.scalar.activation(weighted_b[:, columns], plain_b[:, columns], ACT.Copy, scale=w[:])
-        sum_b = plain_b
+        own_a = held.tile([P, H], F32, name="own_a")
+        nc.vector.tensor_copy(own_a[:], plain_a[:, 0:H])
 
-        for m in range(MN // 2):
-            sum_a = add_neighbour(plain_a, sum_a, m, two)
-        for m in range(MN // 2):
-            sum_b = add_neighbour(weighted_b, sum_b, m, whole)
-            sum_a = add_neighbour(plain_a, sum_a, MN // 2 + m, whole)
-        result_a = held.tile([P, H], F32, name="result_a")
+        sum_a0 = add_neighbour(plain_a, own_a, 0, whole)
+        sum_a1 = add_neighbour(plain_a, own_a, 1, whole)
+        sum_a0 = add_neighbour(plain_a, sum_a0, 2, whole)
+        sum_b = add_neighbour(weighted_b, plain_b, 0, whole)
+        sum_a1 = add_neighbour(plain_a, sum_a1, 3, whole)
+        sum_b = add_neighbour(weighted_b, sum_b, 1, two)
+
         halves = (slice(0, H // 2), slice(H // 2, H))
-        for nodes in halves:
-            nc.scalar.activation(result_a[:, nodes], sum_a[:, nodes], ACT.Copy, scale=w[:])
+        mixed = [psum.tile([P, H // 2], F32, name=f"mixed_{half}") for half in range(2)]
+        for nodes, bank in zip(halves, mixed):
+            nc.tensor.matmul(bank[:], diagonal_rest[:], own_a[:, nodes], start=True, stop=False)
+            nc.tensor.matmul(bank[:], diagonal_w[:], sum_a0[:, nodes], start=False, stop=False)
+        result_a = held.tile([P, H], F32, name="result_a")
+        for nodes, bank in zip(halves, mixed):
+            nc.tensor.matmul(bank[:], diagonal_w[:], sum_a1[:, nodes], start=False, stop=True)
+            nc.scalar.activation(result_a[:, nodes], bank[:], ACT.Copy)
             nc.scalar.dma_start(out[0:P, nodes], result_a[:, nodes])
         sum_b = add_neighbour(weighted_b, sum_b, MN - 2, two)
         sum_b = add_neighbour(weighted_b, sum_b, MN - 1, tapered)

@@ -44,15 +44,15 @@ def tile_capsulenet_kernel(tc, t, raw_param, offs, out):
         nc.scalar.activation(p[:], raw[:], ACT.Sigmoid)
         w = held.tile([P, 1], F32, name="w")
         nc.scalar.activation(w[:], p[:], ACT.Copy, scale=slope, bias=1.0 / KC)
-        weighted_b = held.tile([P, S], F32, name="weighted_b")
-        for columns in (left, right):
-            nc.scalar.activation(weighted_b[:, columns], plain_b[:, columns], ACT.Copy, scale=w[:])
         rest = held.tile([P, 1], F32, name="rest")
         nc.scalar.activation(rest[:], p[:], ACT.Copy, scale=-2.0 * slope, bias=1.0 - 2.0 / KC)
         diagonal_w = held.tile([P, P], F32, name="diagonal_w")
         nc.scalar.activation(diagonal_w[:], identity[:], ACT.Copy, scale=w[:])
         diagonal_rest = held.tile([P, P], F32, name="diagonal_rest")
         nc.scalar.activation(diagonal_rest[:], identity[:], ACT.Copy, scale=rest[:])
+        weighted_b = held.tile([P, S], F32, name="weighted_b")
+        for columns in (left, right):
+            nc.scalar.activation(weighted_b[:, columns], plain_b[:, columns], ACT.Copy, scale=w[:])
 
         def add_neighbour(window, so_far, m, widths):
             total = sums.tile([P, H], F32, name="total")
@@ -83,6 +83,7 @@ def tile_capsulenet_kernel(tc, t, raw_param, offs, out):
         mixed = [psum.tile([P, H // 2], F32, name=f"mixed_{half}") for half in range(2)]
         for nodes, bank in zip(halves, mixed):
             nc.tensor.matmul(bank[:], diagonal_rest[:], own_a[:, nodes], start=True, stop=False)
+        for nodes, bank in zip(halves, mixed):
             nc.tensor.matmul(bank[:], diagonal_w[:], sum_a0[:, nodes], start=False, stop=False)
         result_a = held.tile([P, H], F32, name="result_a")
         for nodes, bank in zip(halves, mixed):

@@ -25,7 +25,6 @@ def tile_capsulenet_kernel(tc, t, raw_param, offs, out):
         tc.psum_pool(name="psum", bufs=1) as psum,
     ):
         raw = held.tile([P, 1], F32, name="raw")
-        nc.scalar.dma_start(raw[:], raw_param.partition_broadcast(P))
         offsets = held.tile([P, N // 16], U16, name="offsets")
         plain_a = held.tile([P, S], F32, name="plain_a")
         plain_b = held.tile([P, S], F32, name="plain_b")
@@ -33,6 +32,7 @@ def tile_capsulenet_kernel(tc, t, raw_param, offs, out):
         for k in range(4):
             columns = slice(k * S // 4, (k + 1) * S // 4)
             nc.sync.dma_start(plain_a[:, columns], t[0:P, columns])
+        nc.sync.dma_start(raw[:], raw_param.partition_broadcast(P))
         nc.sync.dma_start(plain_b[:, left], t[P:C, left])
         nc.sync.dma_start(plain_b[:, right], t[P:C, right])
 

@@ -44,15 +44,15 @@ def tile_capsulenet_kernel(tc, t, raw_param, offs, out):
         nc.scalar.activation(p[:], raw[:], ACT.Sigmoid)
         w = held.tile([P, 1], F32, name="w")
         nc.scalar.activation(w[:], p[:], ACT.Copy, scale=slope, bias=1.0 / KC)
+        weighted_b = held.tile([P, S], F32, name="weighted_b")
+        for columns in (left, right):
+            nc.scalar.activation(weighted_b[:, columns], plain_b[:, columns], ACT.Copy, scale=w[:])
         rest = held.tile([P, 1], F32, name="rest")
         nc.scalar.activation(rest[:], p[:], ACT.Copy, scale=-2.0 * slope, bias=1.0 - 2.0 / KC)
         diagonal_w = held.tile([P, P], F32, name="diagonal_w")
         nc.scalar.activation(diagonal_w[:], identity[:], ACT.Copy, scale=w[:])
         diagonal_rest = held.tile([P, P], F32, name="diagonal_rest")
         nc.scalar.activation(diagonal_rest[:], identity[:], ACT.Copy, scale=rest[:])
-        weighted_b = held.tile([P, S], F32, name="weighted_b")
-        for columns in (left, right):
-            nc.scalar.activation(weighted_b[:, columns], plain_b[:, columns], ACT.Copy, scale=w[:])
 
         def add_neighbour(window, so_far, m, widths):
             total = sums.tile([P, H], F32, name="total")

@@ -70,7 +70,9 @@ def tile_capsulenet_kernel(tc, t, raw_param, offs, out):
         tapered = (H // 2, H // 4, H // 4)
 
         own_a = held.tile([P, H], F32, name="own_a")
-        nc.vector.tensor_copy(own_a[:], plain_a[:, 0:H])
+        for k in range(2):
+            columns = slice(k * S // 4, (k + 1) * S // 4)
+            nc.vector.tensor_copy(own_a[:, columns], plain_a[:, columns])
 
         sum_a0 = add_neighbour(plain_a, own_a, 0, whole)
         sum_a1 = add_neighbour(plain_a, own_a, 1, whole)

@@ -31,7 +31,8 @@ def tile_capsulenet_kernel(tc, t, raw_param, offs, out):
         nc.sync.dma_start(offsets[:], offs)
         for k in range(4):
             columns = slice(k * S // 4, (k + 1) * S // 4)
-            nc.sync.dma_start(plain_a[:, columns], t[0:P, columns])
+            queue = nc.sync if k % 2 == 0 else nc.scalar
+            queue.dma_start(plain_a[:, columns], t[0:P, columns])
         nc.sync.dma_start(raw[:], raw_param.partition_broadcast(P))
         nc.sync.dma_start(plain_b[:, left], t[P:C, left])
         nc.sync.dma_start(plain_b[:, right], t[P:C, right])

import concourse.mybir as mybir
from concourse.masks import make_identity

F32 = mybir.dt.float32
U16 = mybir.dt.uint16
ADD = mybir.AluOpType.add
ACT = mybir.ActivationFunctionType

P = 128
C = 256
S = 1024
H = 512
MN = 4
KC = 8
N = MN * H
FLOPS = C * H * (MN + 2)


def tile_capsulenet_kernel(tc, t, raw_param, offs, out):
    nc = tc.nc
    left, right = slice(0, S // 2), slice(S // 2, S)
    with (
        tc.tile_pool(name="held", bufs=1) as held,
        tc.tile_pool(name="sums", bufs=6) as sums,
        tc.psum_pool(name="psum", bufs=1) as psum,
    ):
        raw = held.tile([P, 1], F32, name="raw")
        offsets = held.tile([P, N // 16], U16, name="offsets")
        plain_a = held.tile([P, S], F32, name="plain_a")
        plain_b = held.tile([P, S], F32, name="plain_b")
        nc.sync.dma_start(offsets[:], offs)
        for k in range(4):
            columns = slice(k * S // 4, (k + 1) * S // 4)
            queue = nc.sync if k % 2 == 0 else nc.scalar
            queue.dma_start(plain_a[:, columns], t[0:P, columns])
        nc.sync.dma_start(raw[:], raw_param.partition_broadcast(P))
        nc.sync.dma_start(plain_b[:, left], t[P:C, left])
        nc.sync.dma_start(plain_b[:, right], t[P:C, right])

        identity = held.tile([P, P], F32, name="identity")
        make_identity(nc, identity[:])

        slope = 1.0 / MN - 1.0 / KC
        p = held.tile([P, 1], F32, name="p")
        nc.scalar.activation(p[:], raw[:], ACT.Sigmoid)
        w = held.tile([P, 1], F32, name="w")
        nc.scalar.activation(w[:], p[:], ACT.Copy, scale=slope, bias=1.0 / KC)
        weighted_b = held.tile([P, S], F32, name="weighted_b")
        for columns in (left, right):
            nc.scalar.activation(weighted_b[:, columns], plain_b[:, columns], ACT.Copy, scale=w[:])
        rest = held.tile([P, 1], F32, name="rest")
        nc.scalar.activation(rest[:], p[:], ACT.Copy, scale=-2.0 * slope, bias=1.0 - 2.0 / KC)
        diagonal_w = held.tile([P, P], F32, name="diagonal_w")
        nc.scalar.activation(diagonal_w[:], identity[:], ACT.Copy, scale=w[:])
        diagonal_rest = held.tile([P, P], F32, name="diagonal_rest")
        nc.scalar.activation(diagonal_rest[:], identity[:], ACT.Copy, scale=rest[:])

        def add_neighbour(window, so_far, m, widths):
            total = sums.tile([P, H], F32, name="total")
            start = 0
            for width in widths:
                nodes = slice(start, start + width)
                first = (m * H + start) // 16
                picked = window[:].indirect(offsets[:, first : first + width // 16])
                nc.vector.tensor_tensor(total[:, nodes], picked, so_far[:, nodes], ADD)
                start += width
            return total

        whole = (H,)
        two = (H // 2, H // 2)
        tapered = (H // 2, H // 4, H // 4)

        own_a = held.tile([P, H], F32, name="own_a")
        for k in range(2):
            columns = slice(k * S // 4, (k + 1) * S // 4)
            nc.vector.tensor_copy(own_a[:, columns], plain_a[:, columns])

        sum_a0 = add_neighbour(plain_a, own_a, 0, whole)
        sum_a1 = add_neighbour(plain_a, own_a, 1, whole)
        sum_a0 = add_neighbour(plain_a, sum_a0, 2, whole)
        sum_b = add_neighbour(weighted_b, plain_b, 0, whole)
        sum_a1 = add_neighbour(plain_a, sum_a1, 3, whole)
        sum_b = add_neighbour(weighted_b, sum_b, 1, two)

        halves = (slice(0, H // 2), slice(H // 2, H))
        mixed = [psum.tile([P, H // 2], F32, name=f"mixed_{half}") for half in range(2)]
        for nodes, bank in zip(halves, mixed):
            nc.tensor.matmul(bank[:], diagonal_rest[:], own_a[:, nodes], start=True, stop=False)
        for nodes, bank in zip(halves, mixed):
            nc.tensor.matmul(bank[:], diagonal_w[:], sum_a0[:, nodes], start=False, stop=False)
        result_a = held.tile([P, H], F32, name="result_a")
        for nodes, bank in zip(halves, mixed):
            nc.tensor.matmul(bank[:], diagonal_w[:], sum_a1[:, nodes], start=False, stop=True)
            nc.scalar.activation(result_a[:, nodes], bank[:], ACT.Copy)
            nc.scalar.dma_start(out[0:P, nodes], result_a[:, nodes])
        sum_b = add_neighbour(weighted_b, sum_b, MN - 2, two)
        sum_b = add_neighbour(weighted_b, sum_b, MN - 1, tapered)
        start = 0
        for width in tapered:
            nodes = slice(start, start + width)
            nc.sync.dma_start(out[P:C, nodes], sum_b[:, nodes])
            start += width
